import numpy as np
import ml_dtypes

BF16 = ml_dtypes.bfloat16


def bf(x):
    return np.asarray(x, np.float32).astype(BF16)


def f32(x):
    return np.asarray(x, np.float32)


def f64(x):
    return np.asarray(x).astype(np.float64)


def striped(idx):
    return np.tile(idx.reshape(-1, 16).T, (8, 1))


V, D, M, F, X, H, K, N = 1024, 128, 128, 128, 10, 512, 4, 2048


def setup_inputs():
    return {
        "table": bf(np.random.standard_normal((D, V))),
        "w": bf(np.random.standard_normal((D, M)) / np.sqrt(D)),
        "dist": f32(np.random.uniform(size=(F, N))),
        "emb_w": bf(np.random.standard_normal((X * F, M)) / np.sqrt(2.0 * X * F)),
        "b": f32(0.1 * np.random.standard_normal((M, 1))),
        "offs": striped(np.concatenate([np.random.permutation(V)[:H] for _ in range(K)])),
    }


def reference(table, w, dist, emb_w, b, offs):
    idx = offs[:16].T.reshape(-1)
    comp = f64(w).T @ f64(table)[:, idx]
    start = np.arange(X, dtype=np.float64) / X
    de = (1.0 - (f64(dist)[None, :, :] - start[:, None, None])) ** 2
    strf = f64(emb_w).T @ de.reshape(X * F, N)
    return comp + strf + f64(b)

@@ -1,0 +1,78 @@
+import concourse.mybir as mybir
+
+BF16, F32, U16 = mybir.dt.bfloat16, mybir.dt.float32, mybir.dt.uint16
+
+P = 128
+TYPES = 1024
+ATOMS = 2048
+PIECE = 512
+PIECES = ATOMS // PIECE
+SHIFTS = 10
+OFFSET_COLUMNS = PIECE // 16
+
+FLOPS = 2 * P * P * ATOMS + 2 * SHIFTS * P * P * ATOMS
+
+
+def on_vector(shift):
+    return shift % 5 in (1, 3)
+
+
+def tile_periodicsettransformer_kernel(tc, table, w, dist, emb_w, b, offs, out):
+    nc = tc.nc
+    square = mybir.ActivationFunctionType.Square
+    identity = mybir.ActivationFunctionType.Identity
+    mult, add = mybir.AluOpType.mult, mybir.AluOpType.add
+
+    with (
+        tc.tile_pool(name="held", bufs=1) as held,
+        tc.tile_pool(name="gaps", bufs=3) as gaps,
+        tc.tile_pool(name="expanded", bufs=8) as expanded,
+        tc.tile_pool(name="results", bufs=PIECES) as results,
+        tc.psum_pool(name="psum", bufs=1) as psum,
+    ):
+        offsets = held.tile([P, ATOMS // 16], U16, name="offsets")
+        nc.sync.dma_start(offsets[:], offs)
+        w_tile = held.tile([P, P], BF16, name="w_tile")
+        nc.sync.dma_start(w_tile[:], w)
+        table_tile = held.tile([P, TYPES], BF16, name="table_tile")
+        nc.sync.dma_start(table_tile[:], table)
+        emb_tile = held.tile([P, SHIFTS, P], BF16, name="emb_tile")
+        nc.sync.dma_start(emb_tile[:], emb_w.rearrange("(i f) m -> f i m", f=P))
+        bias = held.tile([P, 1], F32, name="bias")
+        nc.sync.dma_start(bias[:], b)
+
+        dist_tiles = []
+        for k in range(PIECES):
+            dist_tile = held.tile([P, PIECE], F32, name=f"dist{k}")
+            nc.scalar.dma_start(dist_tile[:], dist[:, k * PIECE : (k + 1) * PIECE])
+            dist_tiles.append(dist_tile)
+
+        banks = []
+        for k in range(PIECES):
+            bank = psum.tile([P, PIECE], F32, name=f"bank{k}")
+            piece_offsets = offsets[:, k * OFFSET_COLUMNS : (k + 1) * OFFSET_COLUMNS]
+            nc.tensor.matmul(
+                bank[:], w_tile[:], table_tile[:].indirect(piece_offsets), start=True, stop=False
+            )
+            banks.append(bank)
+
+        for k in range(PIECES):
+            for i in range(SHIFTS):
+                top = 1.0 + i / 10
+                de = expanded.tile([P, PIECE], BF16, name="de")
+                if on_vector(i):
+                    gap = gaps.tile([P, PIECE], F32, name="gap")
+                    nc.vector.tensor_scalar_sub(gap[:], dist_tiles[k][:], top)
+                    nc.vector.tensor_tensor(de[:], gap[:], gap[:], mult)
+                else:
+                    nc.scalar.activation(de[:], dist_tiles[k][:], square, bias=top, scale=-1.0)
+                nc.tensor.matmul(
+                    banks[k][:], emb_tile[:, i, :], de[:], start=False, stop=(i == SHIFTS - 1)
+                )
+
+            result = results.tile([P, PIECE], F32, name="result")
+            if k % 2 == 0:
+                nc.scalar.activation(result[:], banks[k][:], identity, bias=bias[:, 0:1])
+            else:
+                nc.vector.tensor_scalar(result[:], banks[k][:], bias[:, 0:1], None, add)
+            nc.sync.dma_start(out[:, k * PIECE : (k + 1) * PIECE], result[:])

@@ -26,7 +26,7 @@ def tile_periodicsettransformer_kernel(tc, table, w, dist, emb_w, b, offs, out):
     with (
         tc.tile_pool(name="held", bufs=1) as held,
         tc.tile_pool(name="gaps", bufs=3) as gaps,
-        tc.tile_pool(name="expanded", bufs=8) as expanded,
+        tc.tile_pool(name="expanded", bufs=PIECES * SHIFTS) as expanded,
         tc.tile_pool(name="results", bufs=PIECES) as results,
         tc.psum_pool(name="psum", bufs=1) as psum,
     ):

@@ -5,10 +5,15 @@ BF16, F32, U16 = mybir.dt.bfloat16, mybir.dt.float32, mybir.dt.uint16
 P = 128
 TYPES = 1024
 ATOMS = 2048
-PIECE = 512
-PIECES = ATOMS // PIECE
 SHIFTS = 10
-OFFSET_COLUMNS = PIECE // 16
+PIECE_STARTS = (0, 512, 1024, 1536, 1792)
+PIECE_WIDTHS = (512, 512, 512, 256, 256)
+PIECES = len(PIECE_WIDTHS)
+WARM_UP = 6
+
+assert all(PIECE_STARTS[k] == sum(PIECE_WIDTHS[:k]) for k in range(PIECES))
+assert sum(PIECE_WIDTHS) == ATOMS
+assert all(start % 32 == 0 for start in PIECE_STARTS)
 
 FLOPS = 2 * P * P * ATOMS + 2 * SHIFTS * P * P * ATOMS
 
@@ -23,6 +28,9 @@ def tile_periodicsettransformer_kernel(tc, table, w, dist, emb_w, b, offs, out):
     identity = mybir.ActivationFunctionType.Identity
     mult, add = mybir.AluOpType.mult, mybir.AluOpType.add
 
+    def columns(k):
+        return slice(PIECE_STARTS[k], PIECE_STARTS[k] + PIECE_WIDTHS[k])
+
     with (
         tc.tile_pool(name="held", bufs=1) as held,
         tc.tile_pool(name="gaps", bufs=3) as gaps,
@@ -30,6 +38,8 @@ def tile_periodicsettransformer_kernel(tc, table, w, dist, emb_w, b, offs, out):
         tc.tile_pool(name="results", bufs=PIECES) as results,
         tc.psum_pool(name="psum", bufs=1) as psum,
     ):
+        dist_tiles = [held.tile([P, PIECE_WIDTHS[k]], F32, name=f"dist{k}") for k in range(PIECES)]
+        nc.sync.dma_start(dist_tiles[0][:], dist[:, columns(0)])
         offsets = held.tile([P, ATOMS // 16], U16, name="offsets")
         nc.sync.dma_start(offsets[:], offs)
         w_tile = held.tile([P, P], BF16, name="w_tile")
@@ -38,30 +48,33 @@ def tile_periodicsettransformer_kernel(tc, table, w, dist, emb_w, b, offs, out):
         nc.sync.dma_start(table_tile[:], table)
         emb_tile = held.tile([P, SHIFTS, P], BF16, name="emb_tile")
         nc.sync.dma_start(emb_tile[:], emb_w.rearrange("(i f) m -> f i m", f=P))
+        for k in range(1, PIECES):
+            nc.sync.dma_start(dist_tiles[k][:], dist[:, columns(k)])
         bias = held.tile([P, 1], F32, name="bias")
         nc.sync.dma_start(bias[:], b)
 
-        dist_tiles = []
-        for k in range(PIECES):
-            dist_tile = held.tile([P, PIECE], F32, name=f"dist{k}")
-            nc.scalar.dma_start(dist_tile[:], dist[:, k * PIECE : (k + 1) * PIECE])
-            dist_tiles.append(dist_tile)
+        ones = held.tile([P, 512], BF16, name="ones")
+        nc.vector.memset(ones[:], 1.0)
+        spare_bank = psum.tile([P, 512], F32, name="spare_bank")
+        for n in range(WARM_UP):
+            nc.tensor.matmul(spare_bank[:], ones[:, 0:P], ones[:], start=True, stop=True)
 
         banks = []
         for k in range(PIECES):
-            bank = psum.tile([P, PIECE], F32, name=f"bank{k}")
-            piece_offsets = offsets[:, k * OFFSET_COLUMNS : (k + 1) * OFFSET_COLUMNS]
+            bank = psum.tile([P, PIECE_WIDTHS[k]], F32, name=f"bank{k}")
+            first = PIECE_STARTS[k] // 16
+            piece_offsets = offsets[:, first : first + PIECE_WIDTHS[k] // 16]
             nc.tensor.matmul(
                 bank[:], w_tile[:], table_tile[:].indirect(piece_offsets), start=True, stop=False
             )
             banks.append(bank)
 
-        for k in range(PIECES):
+        def expand(k):
             for i in range(SHIFTS):
                 top = 1.0 + i / 10
-                de = expanded.tile([P, PIECE], BF16, name="de")
+                de = expanded.tile([P, PIECE_WIDTHS[k]], BF16, name="de")
                 if on_vector(i):
-                    gap = gaps.tile([P, PIECE], F32, name="gap")
+                    gap = gaps.tile([P, PIECE_WIDTHS[k]], F32, name="gap")
                     nc.vector.tensor_scalar_sub(gap[:], dist_tiles[k][:], top)
                     nc.vector.tensor_tensor(de[:], gap[:], gap[:], mult)
                 else:
@@ -70,9 +83,16 @@ def tile_periodicsettransformer_kernel(tc, table, w, dist, emb_w, b, offs, out):
                     banks[k][:], emb_tile[:, i, :], de[:], start=False, stop=(i == SHIFTS - 1)
                 )
 
-            result = results.tile([P, PIECE], F32, name="result")
+        def evict(k):
+            result = results.tile([P, PIECE_WIDTHS[k]], F32, name="result")
             if k % 2 == 0:
-                nc.scalar.activation(result[:], banks[k][:], identity, bias=bias[:, 0:1])
-            else:
                 nc.vector.tensor_scalar(result[:], banks[k][:], bias[:, 0:1], None, add)
-            nc.sync.dma_start(out[:, k * PIECE : (k + 1) * PIECE], result[:])
+            else:
+                nc.scalar.activation(result[:], banks[k][:], identity, bias=bias[:, 0:1])
+            nc.sync.dma_start(out[:, columns(k)], result[:])
+
+        for k in range(PIECES):
+            expand(k)
+            if k > 0:
+                evict(k - 1)
+        evict(PIECES - 1)

@@ -9,7 +9,7 @@ SHIFTS = 10
 PIECE_STARTS = (0, 512, 1024, 1536, 1792)
 PIECE_WIDTHS = (512, 512, 512, 256, 256)
 PIECES = len(PIECE_WIDTHS)
-WARM_UP = 6
+WARM_UP = 17
 
 assert all(PIECE_STARTS[k] == sum(PIECE_WIDTHS[:k]) for k in range(PIECES))
 assert sum(PIECE_WIDTHS) == ATOMS
@@ -17,9 +17,11 @@ assert all(start % 32 == 0 for start in PIECE_STARTS)
 
 FLOPS = 2 * P * P * ATOMS + 2 * SHIFTS * P * P * ATOMS
 
+VECTOR_SHIFTS = (2, 4, 6, 8)
 
-def on_vector(shift):
-    return shift % 5 in (1, 3)
+
+def top(i):
+    return 1.0 + i / 10
 
 
 def tile_periodicsettransformer_kernel(tc, table, w, dist, emb_w, b, offs, out):
@@ -33,7 +35,7 @@ def tile_periodicsettransformer_kernel(tc, table, w, dist, emb_w, b, offs, out):
 
     with (
         tc.tile_pool(name="held", bufs=1) as held,
-        tc.tile_pool(name="gaps", bufs=3) as gaps,
+        tc.tile_pool(name="gaps", bufs=2 * len(VECTOR_SHIFTS)) as gaps,
         tc.tile_pool(name="expanded", bufs=PIECES * SHIFTS) as expanded,
         tc.tile_pool(name="results", bufs=PIECES) as results,
         tc.psum_pool(name="psum", bufs=1) as psum,
@@ -46,18 +48,19 @@ def tile_periodicsettransformer_kernel(tc, table, w, dist, emb_w, b, offs, out):
         nc.sync.dma_start(w_tile[:], w)
         table_tile = held.tile([P, TYPES], BF16, name="table_tile")
         nc.sync.dma_start(table_tile[:], table)
+        nc.sync.dma_start(dist_tiles[1][:], dist[:, columns(1)])
         emb_tile = held.tile([P, SHIFTS, P], BF16, name="emb_tile")
         nc.sync.dma_start(emb_tile[:], emb_w.rearrange("(i f) m -> f i m", f=P))
-        for k in range(1, PIECES):
+        for k in range(2, PIECES):
             nc.sync.dma_start(dist_tiles[k][:], dist[:, columns(k)])
         bias = held.tile([P, 1], F32, name="bias")
         nc.sync.dma_start(bias[:], b)
 
-        ones = held.tile([P, 512], BF16, name="ones")
+        ones = held.tile([P, P], BF16, name="ones")
         nc.vector.memset(ones[:], 1.0)
-        spare_bank = psum.tile([P, 512], F32, name="spare_bank")
+        spare_bank = psum.tile([P, P], F32, name="spare_bank")
         for n in range(WARM_UP):
-            nc.tensor.matmul(spare_bank[:], ones[:, 0:P], ones[:], start=True, stop=True)
+            nc.tensor.matmul(spare_bank[:], ones[:], ones[:], start=True, stop=True)
 
         banks = []
         for k in range(PIECES):
@@ -69,16 +72,21 @@ def tile_periodicsettransformer_kernel(tc, table, w, dist, emb_w, b, offs, out):
             )
             banks.append(bank)
 
+        gap_tiles = {}
+
+        def subtract(k, i):
+            gap_tiles[k, i] = gaps.tile([P, PIECE_WIDTHS[k]], F32, name="gap")
+            nc.vector.tensor_scalar_sub(gap_tiles[k, i][:], dist_tiles[k][:], top(i))
+
         def expand(k):
             for i in range(SHIFTS):
-                top = 1.0 + i / 10
                 de = expanded.tile([P, PIECE_WIDTHS[k]], BF16, name="de")
-                if on_vector(i):
-                    gap = gaps.tile([P, PIECE_WIDTHS[k]], F32, name="gap")
-                    nc.vector.tensor_scalar_sub(gap[:], dist_tiles[k][:], top)
-                    nc.vector.tensor_tensor(de[:], gap[:], gap[:], mult)
+                if i in VECTOR_SHIFTS:
+                    nc.vector.tensor_tensor(de[:], gap_tiles[k, i][:], gap_tiles[k, i][:], mult)
+                    if k + 1 < PIECES:
+                        subtract(k + 1, i)
                 else:
-                    nc.scalar.activation(de[:], dist_tiles[k][:], square, bias=top, scale=-1.0)
+                    nc.scalar.activation(de[:], dist_tiles[k][:], square, bias=top(i), scale=-1.0)
                 nc.tensor.matmul(
                     banks[k][:], emb_tile[:, i, :], de[:], start=False, stop=(i == SHIFTS - 1)
                 )
@@ -91,8 +99,15 @@ def tile_periodicsettransformer_kernel(tc, table, w, dist, emb_w, b, offs, out):
                 nc.scalar.activation(result[:], banks[k][:], identity, bias=bias[:, 0:1])
             nc.sync.dma_start(out[:, columns(k)], result[:])
 
-        for k in range(PIECES):
-            expand(k)
-            if k > 0:
-                evict(k - 1)
-        evict(PIECES - 1)
+        for i in VECTOR_SHIFTS:
+            subtract(0, i)
+        expand(0)
+        expand(1)
+        evict(0)
+        expand(2)
+        evict(1)
+        expand(3)
+        expand(4)
+        evict(2)
+        evict(3)
+        evict(4)

@@ -5,17 +5,14 @@ BF16, F32, U16 = mybir.dt.bfloat16, mybir.dt.float32, mybir.dt.uint16
 P = 128
 TYPES = 1024
 ATOMS = 2048
+PIECE = 512
+PIECES = ATOMS // PIECE
 SHIFTS = 10
-PIECE_STARTS = (0, 512, 1024, 1536, 1792)
-PIECE_WIDTHS = (512, 512, 512, 256, 256)
-PIECES = len(PIECE_WIDTHS)
-WARM_UP = 17
-
-assert all(PIECE_STARTS[k] == sum(PIECE_WIDTHS[:k]) for k in range(PIECES))
-assert sum(PIECE_WIDTHS) == ATOMS
-assert all(start % 32 == 0 for start in PIECE_STARTS)
+OFFSET_COLUMNS = PIECE // 16
+WARM_UP = 6
 
 FLOPS = 2 * P * P * ATOMS + 2 * SHIFTS * P * P * ATOMS
+
 
 VECTOR_SHIFTS = (2, 4, 6, 8)
 
@@ -30,9 +27,6 @@ def tile_periodicsettransformer_kernel(tc, table, w, dist, emb_w, b, offs, out):
     identity = mybir.ActivationFunctionType.Identity
     mult, add = mybir.AluOpType.mult, mybir.AluOpType.add
 
-    def columns(k):
-        return slice(PIECE_STARTS[k], PIECE_STARTS[k] + PIECE_WIDTHS[k])
-
     with (
         tc.tile_pool(name="held", bufs=1) as held,
         tc.tile_pool(name="gaps", bufs=2 * len(VECTOR_SHIFTS)) as gaps,
@@ -40,33 +34,32 @@ def tile_periodicsettransformer_kernel(tc, table, w, dist, emb_w, b, offs, out):
         tc.tile_pool(name="results", bufs=PIECES) as results,
         tc.psum_pool(name="psum", bufs=1) as psum,
     ):
-        dist_tiles = [held.tile([P, PIECE_WIDTHS[k]], F32, name=f"dist{k}") for k in range(PIECES)]
-        nc.sync.dma_start(dist_tiles[0][:], dist[:, columns(0)])
+        dist_tiles = [held.tile([P, PIECE], F32, name=f"dist{k}") for k in range(PIECES)]
+        nc.sync.dma_start(dist_tiles[0][:], dist[:, 0:PIECE])
         offsets = held.tile([P, ATOMS // 16], U16, name="offsets")
         nc.sync.dma_start(offsets[:], offs)
         w_tile = held.tile([P, P], BF16, name="w_tile")
         nc.sync.dma_start(w_tile[:], w)
         table_tile = held.tile([P, TYPES], BF16, name="table_tile")
         nc.sync.dma_start(table_tile[:], table)
-        nc.sync.dma_start(dist_tiles[1][:], dist[:, columns(1)])
+        nc.sync.dma_start(dist_tiles[1][:], dist[:, PIECE : 2 * PIECE])
         emb_tile = held.tile([P, SHIFTS, P], BF16, name="emb_tile")
         nc.sync.dma_start(emb_tile[:], emb_w.rearrange("(i f) m -> f i m", f=P))
         for k in range(2, PIECES):
-            nc.sync.dma_start(dist_tiles[k][:], dist[:, columns(k)])
+            nc.sync.dma_start(dist_tiles[k][:], dist[:, k * PIECE : (k + 1) * PIECE])
         bias = held.tile([P, 1], F32, name="bias")
         nc.sync.dma_start(bias[:], b)
 
-        ones = held.tile([P, P], BF16, name="ones")
+        ones = held.tile([P, PIECE], BF16, name="ones")
         nc.vector.memset(ones[:], 1.0)
-        spare_bank = psum.tile([P, P], F32, name="spare_bank")
+        spare_bank = psum.tile([P, PIECE], F32, name="spare_bank")
         for n in range(WARM_UP):
-            nc.tensor.matmul(spare_bank[:], ones[:], ones[:], start=True, stop=True)
+            nc.tensor.matmul(spare_bank[:], ones[:, 0:P], ones[:], start=True, stop=True)
 
         banks = []
         for k in range(PIECES):
-            bank = psum.tile([P, PIECE_WIDTHS[k]], F32, name=f"bank{k}")
-            first = PIECE_STARTS[k] // 16
-            piece_offsets = offsets[:, first : first + PIECE_WIDTHS[k] // 16]
+            bank = psum.tile([P, PIECE], F32, name=f"bank{k}")
+            piece_offsets = offsets[:, k * OFFSET_COLUMNS : (k + 1) * OFFSET_COLUMNS]
             nc.tensor.matmul(
                 bank[:], w_tile[:], table_tile[:].indirect(piece_offsets), start=True, stop=False
             )
@@ -75,12 +68,12 @@ def tile_periodicsettransformer_kernel(tc, table, w, dist, emb_w, b, offs, out):
         gap_tiles = {}
 
         def subtract(k, i):
-            gap_tiles[k, i] = gaps.tile([P, PIECE_WIDTHS[k]], F32, name="gap")
+            gap_tiles[k, i] = gaps.tile([P, PIECE], F32, name="gap")
             nc.vector.tensor_scalar_sub(gap_tiles[k, i][:], dist_tiles[k][:], top(i))
 
         def expand(k):
             for i in range(SHIFTS):
-                de = expanded.tile([P, PIECE_WIDTHS[k]], BF16, name="de")
+                de = expanded.tile([P, PIECE], BF16, name="de")
                 if i in VECTOR_SHIFTS:
                     nc.vector.tensor_tensor(de[:], gap_tiles[k, i][:], gap_tiles[k, i][:], mult)
                     if k + 1 < PIECES:
@@ -92,22 +85,17 @@ def tile_periodicsettransformer_kernel(tc, table, w, dist, emb_w, b, offs, out):
                 )
 
         def evict(k):
-            result = results.tile([P, PIECE_WIDTHS[k]], F32, name="result")
+            result = results.tile([P, PIECE], F32, name="result")
             if k % 2 == 0:
-                nc.vector.tensor_scalar(result[:], banks[k][:], bias[:, 0:1], None, add)
-            else:
                 nc.scalar.activation(result[:], banks[k][:], identity, bias=bias[:, 0:1])
-            nc.sync.dma_start(out[:, columns(k)], result[:])
+            else:
+                nc.vector.tensor_scalar(result[:], banks[k][:], bias[:, 0:1], None, add)
+            nc.sync.dma_start(out[:, k * PIECE : (k + 1) * PIECE], result[:])
 
         for i in VECTOR_SHIFTS:
             subtract(0, i)
-        expand(0)
-        expand(1)
-        evict(0)
-        expand(2)
-        evict(1)
-        expand(3)
-        expand(4)
-        evict(2)
-        evict(3)
-        evict(4)
+        for k in range(PIECES):
+            expand(k)
+            if k > 0:
+                evict(k - 1)
+        evict(PIECES - 1)

@@ -9,7 +9,6 @@ PIECE = 512
 PIECES = ATOMS // PIECE
 SHIFTS = 10
 OFFSET_COLUMNS = PIECE // 16
-WARM_UP = 6
 
 FLOPS = 2 * P * P * ATOMS + 2 * SHIFTS * P * P * ATOMS
 
@@ -49,12 +48,6 @@ def tile_periodicsettransformer_kernel(tc, table, w, dist, emb_w, b, offs, out):
             nc.sync.dma_start(dist_tiles[k][:], dist[:, k * PIECE : (k + 1) * PIECE])
         bias = held.tile([P, 1], F32, name="bias")
         nc.sync.dma_start(bias[:], b)
-
-        ones = held.tile([P, PIECE], BF16, name="ones")
-        nc.vector.memset(ones[:], 1.0)
-        spare_bank = psum.tile([P, PIECE], F32, name="spare_bank")
-        for n in range(WARM_UP):
-            nc.tensor.matmul(spare_bank[:], ones[:, 0:P], ones[:], start=True, stop=True)
 
         banks = []
         for k in range(PIECES):

@@ -6,9 +6,10 @@ P = 128
 TYPES = 1024
 ATOMS = 2048
 PIECE = 512
+HALF = PIECE // 2
 PIECES = ATOMS // PIECE
+LAST = PIECES - 1
 SHIFTS = 10
-OFFSET_COLUMNS = PIECE // 16
 
 FLOPS = 2 * P * P * ATOMS + 2 * SHIFTS * P * P * ATOMS
 
@@ -20,6 +21,12 @@ def top(i):
     return 1.0 + i / 10
 
 
+def bank_columns(k):
+    if k < LAST:
+        return [(0, PIECE)]
+    return [(0, HALF), (HALF, PIECE)]
+
+
 def tile_periodicsettransformer_kernel(tc, table, w, dist, emb_w, b, offs, out):
     nc = tc.nc
     square = mybir.ActivationFunctionType.Square
@@ -29,8 +36,8 @@ def tile_periodicsettransformer_kernel(tc, table, w, dist, emb_w, b, offs, out):
     with (
         tc.tile_pool(name="held", bufs=1) as held,
         tc.tile_pool(name="gaps", bufs=2 * len(VECTOR_SHIFTS)) as gaps,
-        tc.tile_pool(name="expanded", bufs=PIECES * SHIFTS) as expanded,
-        tc.tile_pool(name="results", bufs=PIECES) as results,
+        tc.tile_pool(name="expanded", bufs=PIECES * SHIFTS + 1) as expanded,
+        tc.tile_pool(name="results", bufs=PIECES + 1) as results,
         tc.psum_pool(name="psum", bufs=1) as psum,
     ):
         dist_tiles = [held.tile([P, PIECE], F32, name=f"dist{k}") for k in range(PIECES)]
@@ -49,14 +56,19 @@ def tile_periodicsettransformer_kernel(tc, table, w, dist, emb_w, b, offs, out):
         bias = held.tile([P, 1], F32, name="bias")
         nc.sync.dma_start(bias[:], b)
 
-        banks = []
+        banks = {}
         for k in range(PIECES):
-            bank = psum.tile([P, PIECE], F32, name=f"bank{k}")
-            piece_offsets = offsets[:, k * OFFSET_COLUMNS : (k + 1) * OFFSET_COLUMNS]
-            nc.tensor.matmul(
-                bank[:], w_tile[:], table_tile[:].indirect(piece_offsets), start=True, stop=False
-            )
-            banks.append(bank)
+            for lo, hi in bank_columns(k):
+                banks[k, lo] = psum.tile([P, PIECE], F32, name=f"bank{k}_{lo}")
+                first = k * PIECE + lo
+                bank_offsets = offsets[:, first // 16 : (first + hi - lo) // 16]
+                nc.tensor.matmul(
+                    banks[k, lo][:, 0 : hi - lo],
+                    w_tile[:],
+                    table_tile[:].indirect(bank_offsets),
+                    start=True,
+                    stop=False,
+                )
 
         gap_tiles = {}
 
@@ -64,31 +76,58 @@ def tile_periodicsettransformer_kernel(tc, table, w, dist, emb_w, b, offs, out):
             gap_tiles[k, i] = gaps.tile([P, PIECE], F32, name="gap")
             nc.vector.tensor_scalar_sub(gap_tiles[k, i][:], dist_tiles[k][:], top(i))
 
-        def expand(k):
-            for i in range(SHIFTS):
-                de = expanded.tile([P, PIECE], BF16, name="de")
+        def expand(k, shifts):
+            for i in shifts:
                 if i in VECTOR_SHIFTS:
+                    de = expanded.tile([P, PIECE], BF16, name="de")
                     nc.vector.tensor_tensor(de[:], gap_tiles[k, i][:], gap_tiles[k, i][:], mult)
-                    if k + 1 < PIECES:
+                    if k < LAST:
                         subtract(k + 1, i)
-                else:
+                    parts = {lo: de[:, lo:hi] for lo, hi in bank_columns(k)}
+                elif i < SHIFTS - 1:
+                    de = expanded.tile([P, PIECE], BF16, name="de")
                     nc.scalar.activation(de[:], dist_tiles[k][:], square, bias=top(i), scale=-1.0)
-                nc.tensor.matmul(
-                    banks[k][:], emb_tile[:, i, :], de[:], start=False, stop=(i == SHIFTS - 1)
-                )
+                    parts = {lo: de[:, lo:hi] for lo, hi in bank_columns(k)}
+                else:
+                    parts = {}
+                    for lo, hi in bank_columns(k):
+                        de = expanded.tile([P, hi - lo], BF16, name="de")
+                        nc.scalar.activation(
+                            de[:], dist_tiles[k][:, lo:hi], square, bias=top(i), scale=-1.0
+                        )
+                        parts[lo] = de[:]
+                for lo, hi in bank_columns(k):
+                    nc.tensor.matmul(
+                        banks[k, lo][:, 0 : hi - lo],
+                        emb_tile[:, i, :],
+                        parts[lo],
+                        start=False,
+                        stop=(i == SHIFTS - 1),
+                    )
+
+        evicted = []
 
         def evict(k):
-            result = results.tile([P, PIECE], F32, name="result")
-            if k % 2 == 0:
-                nc.scalar.activation(result[:], banks[k][:], identity, bias=bias[:, 0:1])
-            else:
-                nc.vector.tensor_scalar(result[:], banks[k][:], bias[:, 0:1], None, add)
-            nc.sync.dma_start(out[:, k * PIECE : (k + 1) * PIECE], result[:])
+            for lo, hi in bank_columns(k):
+                result = results.tile([P, hi - lo], F32, name="result")
+                if len(evicted) % 2 == 0:
+                    nc.scalar.activation(
+                        result[:], banks[k, lo][:, 0 : hi - lo], identity, bias=bias[:, 0:1]
+                    )
+                else:
+                    nc.vector.tensor_scalar(
+                        result[:], banks[k, lo][:, 0 : hi - lo], bias[:, 0:1], None, add
+                    )
+                evicted.append((k, lo))
+                nc.sync.dma_start(out[:, k * PIECE + lo : k * PIECE + hi], result[:])
 
         for i in VECTOR_SHIFTS:
             subtract(0, i)
-        for k in range(PIECES):
-            expand(k)
+        for k in range(LAST):
+            expand(k, range(SHIFTS))
             if k > 0:
                 evict(k - 1)
-        evict(PIECES - 1)
+        expand(LAST, range(SHIFTS // 2))
+        evict(LAST - 1)
+        expand(LAST, range(SHIFTS // 2, SHIFTS))
+        evict(LAST)

@@ -76,8 +76,8 @@ def tile_periodicsettransformer_kernel(tc, table, w, dist, emb_w, b, offs, out):
             gap_tiles[k, i] = gaps.tile([P, PIECE], F32, name="gap")
             nc.vector.tensor_scalar_sub(gap_tiles[k, i][:], dist_tiles[k][:], top(i))
 
-        def expand(k, shifts):
-            for i in shifts:
+        def expand(k):
+            for i in range(SHIFTS):
                 if i in VECTOR_SHIFTS:
                     de = expanded.tile([P, PIECE], BF16, name="de")
                     nc.vector.tensor_tensor(de[:], gap_tiles[k, i][:], gap_tiles[k, i][:], mult)
@@ -123,11 +123,8 @@ def tile_periodicsettransformer_kernel(tc, table, w, dist, emb_w, b, offs, out):
 
         for i in VECTOR_SHIFTS:
             subtract(0, i)
-        for k in range(LAST):
-            expand(k, range(SHIFTS))
+        for k in range(PIECES):
+            expand(k)
             if k > 0:
                 evict(k - 1)
-        expand(LAST, range(SHIFTS // 2))
-        evict(LAST - 1)
-        expand(LAST, range(SHIFTS // 2, SHIFTS))
         evict(LAST)

@@ -7,6 +7,7 @@ TYPES = 1024
 ATOMS = 2048
 PIECE = 512
 HALF = PIECE // 2
+HALVES = ((0, HALF), (HALF, PIECE))
 PIECES = ATOMS // PIECE
 LAST = PIECES - 1
 SHIFTS = 10
@@ -24,7 +25,7 @@ def top(i):
 def bank_columns(k):
     if k < LAST:
         return [(0, PIECE)]
-    return [(0, HALF), (HALF, PIECE)]
+    return list(HALVES)
 
 
 def tile_periodicsettransformer_kernel(tc, table, w, dist, emb_w, b, offs, out):
@@ -41,7 +42,8 @@ def tile_periodicsettransformer_kernel(tc, table, w, dist, emb_w, b, offs, out):
         tc.psum_pool(name="psum", bufs=1) as psum,
     ):
         dist_tiles = [held.tile([P, PIECE], F32, name=f"dist{k}") for k in range(PIECES)]
-        nc.sync.dma_start(dist_tiles[0][:], dist[:, 0:PIECE])
+        for lo, hi in HALVES:
+            nc.sync.dma_start(dist_tiles[0][:, lo:hi], dist[:, lo:hi])
         offsets = held.tile([P, ATOMS // 16], U16, name="offsets")
         nc.sync.dma_start(offsets[:], offs)
         w_tile = held.tile([P, P], BF16, name="w_tile")
@@ -76,6 +78,15 @@ def tile_periodicsettransformer_kernel(tc, table, w, dist, emb_w, b, offs, out):
             gap_tiles[k, i] = gaps.tile([P, PIECE], F32, name="gap")
             nc.vector.tensor_scalar_sub(gap_tiles[k, i][:], dist_tiles[k][:], top(i))
 
+        def subtract_first_piece():
+            for i in VECTOR_SHIFTS:
+                gap_tiles[0, i] = gaps.tile([P, PIECE], F32, name="gap")
+            for lo, hi in HALVES:
+                for i in VECTOR_SHIFTS:
+                    nc.vector.tensor_scalar_sub(
+                        gap_tiles[0, i][:, lo:hi], dist_tiles[0][:, lo:hi], top(i)
+                    )
+
         def expand(k):
             for i in range(SHIFTS):
                 if i in VECTOR_SHIFTS:
@@ -84,6 +95,13 @@ def tile_periodicsettransformer_kernel(tc, table, w, dist, emb_w, b, offs, out):
                     if k < LAST:
                         subtract(k + 1, i)
                     parts = {lo: de[:, lo:hi] for lo, hi in bank_columns(k)}
+                elif k == 0 and i == 0:
+                    de = expanded.tile([P, PIECE], BF16, name="de")
+                    for lo, hi in HALVES:
+                        nc.scalar.activation(
+                            de[:, lo:hi], dist_tiles[k][:, lo:hi], square, bias=top(i), scale=-1.0
+                        )
+                    parts = {0: de[:]}
                 elif i < SHIFTS - 1:
                     de = expanded.tile([P, PIECE], BF16, name="de")
                     nc.scalar.activation(de[:], dist_tiles[k][:], square, bias=top(i), scale=-1.0)
@@ -121,8 +139,7 @@ def tile_periodicsettransformer_kernel(tc, table, w, dist, emb_w, b, offs, out):
                 evicted.append((k, lo))
                 nc.sync.dma_start(out[:, k * PIECE + lo : k * PIECE + hi], result[:])
 
-        for i in VECTOR_SHIFTS:
-            subtract(0, i)
+        subtract_first_piece()
         for k in range(PIECES):
             expand(k)
             if k > 0:

@@ -50,10 +50,9 @@ def tile_periodicsettransformer_kernel(tc, table, w, dist, emb_w, b, offs, out):
         nc.sync.dma_start(w_tile[:], w)
         table_tile = held.tile([P, TYPES], BF16, name="table_tile")
         nc.sync.dma_start(table_tile[:], table)
-        nc.sync.dma_start(dist_tiles[1][:], dist[:, PIECE : 2 * PIECE])
         emb_tile = held.tile([P, SHIFTS, P], BF16, name="emb_tile")
         nc.sync.dma_start(emb_tile[:], emb_w.rearrange("(i f) m -> f i m", f=P))
-        for k in range(2, PIECES):
+        for k in range(1, PIECES):
             nc.sync.dma_start(dist_tiles[k][:], dist[:, k * PIECE : (k + 1) * PIECE])
         bias = held.tile([P, 1], F32, name="bias")
         nc.sync.dma_start(bias[:], b)
@@ -92,8 +91,6 @@ def tile_periodicsettransformer_kernel(tc, table, w, dist, emb_w, b, offs, out):
                 if i in VECTOR_SHIFTS:
                     de = expanded.tile([P, PIECE], BF16, name="de")
                     nc.vector.tensor_tensor(de[:], gap_tiles[k, i][:], gap_tiles[k, i][:], mult)
-                    if k < LAST:
-                        subtract(k + 1, i)
                     parts = {lo: de[:, lo:hi] for lo, hi in bank_columns(k)}
                 elif k == 0 and i == 0:
                     de = expanded.tile([P, PIECE], BF16, name="de")
@@ -142,6 +139,9 @@ def tile_periodicsettransformer_kernel(tc, table, w, dist, emb_w, b, offs, out):
         subtract_first_piece()
         for k in range(PIECES):
             expand(k)
+            if k < LAST:
+                for i in VECTOR_SHIFTS:
+                    subtract(k + 1, i)
             if k > 0:
                 evict(k - 1)
         evict(LAST)

@@ -15,7 +15,7 @@ SHIFTS = 10
 FLOPS = 2 * P * P * ATOMS + 2 * SHIFTS * P * P * ATOMS
 
 
-VECTOR_SHIFTS = (2, 4, 6, 8)
+VECTOR_SHIFTS = (3, 4, 7, 8)
 
 
 def top(i):
@@ -36,8 +36,9 @@ def tile_periodicsettransformer_kernel(tc, table, w, dist, emb_w, b, offs, out):
 
     with (
         tc.tile_pool(name="held", bufs=1) as held,
-        tc.tile_pool(name="gaps", bufs=2 * len(VECTOR_SHIFTS)) as gaps,
-        tc.tile_pool(name="expanded", bufs=PIECES * SHIFTS + 1) as expanded,
+        tc.tile_pool(name="gaps", bufs=2) as gaps,
+        tc.tile_pool(name="squares", bufs=PIECES * (SHIFTS - len(VECTOR_SHIFTS)) + 1) as squares,
+        tc.tile_pool(name="products", bufs=PIECES) as products,
         tc.tile_pool(name="results", bufs=PIECES + 1) as results,
         tc.psum_pool(name="psum", bufs=1) as psum,
     ):
@@ -73,40 +74,39 @@ def tile_periodicsettransformer_kernel(tc, table, w, dist, emb_w, b, offs, out):
 
         gap_tiles = {}
 
-        def subtract(k, i):
-            gap_tiles[k, i] = gaps.tile([P, PIECE], F32, name="gap")
-            nc.vector.tensor_scalar_sub(gap_tiles[k, i][:], dist_tiles[k][:], top(i))
-
-        def subtract_first_piece():
-            for i in VECTOR_SHIFTS:
-                gap_tiles[0, i] = gaps.tile([P, PIECE], F32, name="gap")
-            for lo, hi in HALVES:
-                for i in VECTOR_SHIFTS:
+        def subtract(k, parts):
+            gap_tiles[k] = gaps.tile([P, len(VECTOR_SHIFTS), PIECE], F32, name="gap")
+            for lo, hi in parts:
+                for n, i in enumerate(VECTOR_SHIFTS):
                     nc.vector.tensor_scalar_sub(
-                        gap_tiles[0, i][:, lo:hi], dist_tiles[0][:, lo:hi], top(i)
+                        gap_tiles[k][:, n, lo:hi], dist_tiles[k][:, lo:hi], top(i)
                     )
 
         def expand(k):
+            product = products.tile([P, len(VECTOR_SHIFTS), PIECE], BF16, name="product")
+            step = 2 if k < LAST else 1
             for i in range(SHIFTS):
                 if i in VECTOR_SHIFTS:
-                    de = expanded.tile([P, PIECE], BF16, name="de")
-                    nc.vector.tensor_tensor(de[:], gap_tiles[k, i][:], gap_tiles[k, i][:], mult)
-                    parts = {lo: de[:, lo:hi] for lo, hi in bank_columns(k)}
+                    n = VECTOR_SHIFTS.index(i)
+                    if n % step == 0:
+                        gap = gap_tiles[k][:, n : n + step, :]
+                        nc.vector.tensor_tensor(product[:, n : n + step, :], gap, gap, mult)
+                    parts = {lo: product[:, n, lo:hi] for lo, hi in bank_columns(k)}
                 elif k == 0 and i == 0:
-                    de = expanded.tile([P, PIECE], BF16, name="de")
+                    de = squares.tile([P, PIECE], BF16, name="de")
                     for lo, hi in HALVES:
                         nc.scalar.activation(
                             de[:, lo:hi], dist_tiles[k][:, lo:hi], square, bias=top(i), scale=-1.0
                         )
                     parts = {0: de[:]}
                 elif i < SHIFTS - 1:
-                    de = expanded.tile([P, PIECE], BF16, name="de")
+                    de = squares.tile([P, PIECE], BF16, name="de")
                     nc.scalar.activation(de[:], dist_tiles[k][:], square, bias=top(i), scale=-1.0)
                     parts = {lo: de[:, lo:hi] for lo, hi in bank_columns(k)}
                 else:
                     parts = {}
                     for lo, hi in bank_columns(k):
-                        de = expanded.tile([P, hi - lo], BF16, name="de")
+                        de = squares.tile([P, hi - lo], BF16, name="de")
                         nc.scalar.activation(
                             de[:], dist_tiles[k][:, lo:hi], square, bias=top(i), scale=-1.0
                         )
@@ -136,12 +136,11 @@ def tile_periodicsettransformer_kernel(tc, table, w, dist, emb_w, b, offs, out):
                 evicted.append((k, lo))
                 nc.sync.dma_start(out[:, k * PIECE + lo : k * PIECE + hi], result[:])
 
-        subtract_first_piece()
+        subtract(0, HALVES)
         for k in range(PIECES):
             expand(k)
             if k < LAST:
-                for i in VECTOR_SHIFTS:
-                    subtract(k + 1, i)
+                subtract(k + 1, [(0, PIECE)])
             if k > 0:
                 evict(k - 1)
         evict(LAST)

import concourse.mybir as mybir

BF16, F32, U16 = mybir.dt.bfloat16, mybir.dt.float32, mybir.dt.uint16

P = 128
TYPES = 1024
ATOMS = 2048
PIECE = 512
HALF = PIECE // 2
HALVES = ((0, HALF), (HALF, PIECE))
PIECES = ATOMS // PIECE
LAST = PIECES - 1
SHIFTS = 10

FLOPS = 2 * P * P * ATOMS + 2 * SHIFTS * P * P * ATOMS


VECTOR_SHIFTS = (3, 4, 7, 8)


def top(i):
    return 1.0 + i / 10


def bank_columns(k):
    if k < LAST:
        return [(0, PIECE)]
    return list(HALVES)


def tile_periodicsettransformer_kernel(tc, table, w, dist, emb_w, b, offs, out):
    nc = tc.nc
    square = mybir.ActivationFunctionType.Square
    identity = mybir.ActivationFunctionType.Identity
    mult, add = mybir.AluOpType.mult, mybir.AluOpType.add

    with (
        tc.tile_pool(name="held", bufs=1) as held,
        tc.tile_pool(name="gaps", bufs=2) as gaps,
        tc.tile_pool(name="squares", bufs=PIECES * (SHIFTS - len(VECTOR_SHIFTS)) + 1) as squares,
        tc.tile_pool(name="products", bufs=PIECES) as products,
        tc.tile_pool(name="results", bufs=PIECES + 1) as results,
        tc.psum_pool(name="psum", bufs=1) as psum,
    ):
        dist_tiles = [held.tile([P, PIECE], F32, name=f"dist{k}") for k in range(PIECES)]
        for lo, hi in HALVES:
            nc.sync.dma_start(dist_tiles[0][:, lo:hi], dist[:, lo:hi])
        offsets = held.tile([P, ATOMS // 16], U16, name="offsets")
        nc.sync.dma_start(offsets[:], offs)
        w_tile = held.tile([P, P], BF16, name="w_tile")
        nc.sync.dma_start(w_tile[:], w)
        table_tile = held.tile([P, TYPES], BF16, name="table_tile")
        nc.sync.dma_start(table_tile[:], table)
        emb_tile = held.tile([P, SHIFTS, P], BF16, name="emb_tile")
        nc.sync.dma_start(emb_tile[:], emb_w.rearrange("(i f) m -> f i m", f=P))
        for k in range(1, PIECES):
            nc.sync.dma_start(dist_tiles[k][:], dist[:, k * PIECE : (k + 1) * PIECE])
        bias = held.tile([P, 1], F32, name="bias")
        nc.sync.dma_start(bias[:], b)

        banks = {}
        for k in range(PIECES):
            for lo, hi in bank_columns(k):
                banks[k, lo] = psum.tile([P, PIECE], F32, name=f"bank{k}_{lo}")
                first = k * PIECE + lo
                bank_offsets = offsets[:, first // 16 : (first + hi - lo) // 16]
                nc.tensor.matmul(
                    banks[k, lo][:, 0 : hi - lo],
                    w_tile[:],
                    table_tile[:].indirect(bank_offsets),
                    start=True,
                    stop=False,
                )

        gap_tiles = {}

        def subtract(k, parts):
            gap_tiles[k] = gaps.tile([P, len(VECTOR_SHIFTS), PIECE], F32, name="gap")
            for lo, hi in parts:
                for n, i in enumerate(VECTOR_SHIFTS):
                    nc.vector.tensor_scalar_sub(
                        gap_tiles[k][:, n, lo:hi], dist_tiles[k][:, lo:hi], top(i)
                    )

        def expand(k):
            product = products.tile([P, len(VECTOR_SHIFTS), PIECE], BF16, name="product")
            step = 2 if k < LAST else 1
            for i in range(SHIFTS):
                if i in VECTOR_SHIFTS:
                    n = VECTOR_SHIFTS.index(i)
                    if n % step == 0:
                        gap = gap_tiles[k][:, n : n + step, :]
                        nc.vector.tensor_tensor(product[:, n : n + step, :], gap, gap, mult)
                    parts = {lo: product[:, n, lo:hi] for lo, hi in bank_columns(k)}
                elif k == 0 and i == 0:
                    de = squares.tile([P, PIECE], BF16, name="de")
                    for lo, hi in HALVES:
                        nc.scalar.activation(
                            de[:, lo:hi], dist_tiles[k][:, lo:hi], square, bias=top(i), scale=-1.0
                        )
                    parts = {0: de[:]}
                elif i < SHIFTS - 1:
                    de = squares.tile([P, PIECE], BF16, name="de")
                    nc.scalar.activation(de[:], dist_tiles[k][:], square, bias=top(i), scale=-1.0)
                    parts = {lo: de[:, lo:hi] for lo, hi in bank_columns(k)}
                else:
                    parts = {}
                    for lo, hi in bank_columns(k):
                        de = squares.tile([P, hi - lo], BF16, name="de")
                        nc.scalar.activation(
                            de[:], dist_tiles[k][:, lo:hi], square, bias=top(i), scale=-1.0
                        )
                        parts[lo] = de[:]
                for lo, hi in bank_columns(k):
                    nc.tensor.matmul(
                        banks[k, lo][:, 0 : hi - lo],
                        emb_tile[:, i, :],
                        parts[lo],
                        start=False,
                        stop=(i == SHIFTS - 1),
                    )

        evicted = []

        def evict(k):
            for lo, hi in bank_columns(k):
                result = results.tile([P, hi - lo], F32, name="result")
                if len(evicted) % 2 == 0:
                    nc.scalar.activation(
                        result[:], banks[k, lo][:, 0 : hi - lo], identity, bias=bias[:, 0:1]
                    )
                else:
                    nc.vector.tensor_scalar(
                        result[:], banks[k, lo][:, 0 : hi - lo], bias[:, 0:1], None, add
                    )
                evicted.append((k, lo))
                nc.sync.dma_start(out[:, k * PIECE + lo : k * PIECE + hi], result[:])

        subtract(0, HALVES)
        for k in range(PIECES):
            expand(k)
            if k < LAST:
                subtract(k + 1, [(0, PIECE)])
            if k > 0:
                evict(k - 1)
        evict(LAST)
